import numpy as np
import ml_dtypes


def mxq(x, axis, fmt="e4m3"):
    dtype, down = {"e4m3": (ml_dtypes.float8_e4m3fn, 7), "e5m2": (ml_dtypes.float8_e5m2, 14)}[fmt]
    v = np.moveaxis(np.asarray(x, np.float32).astype(ml_dtypes.bfloat16).astype(np.float64), axis, -1)
    blocks = v.reshape(v.shape[:-1] + (-1, 32))
    amax = np.abs(blocks).max(-1, keepdims=True)
    byte = np.maximum(np.where(amax > 0, np.frexp(amax)[1] - 1 + 127, 0) - down, 1)
    scale = np.exp2(byte - 127.0)
    codes = (blocks / scale).astype(np.float32).astype(dtype).astype(np.float64)
    return np.moveaxis((codes * scale).reshape(v.shape), -1, axis)


WIDE = False


def mx_kscale(k):
    if not WIDE:
        return np.ones(k)
    levels = np.array([10, -10, 5, -5, 0])
    if k % 512:
        return np.exp2(np.random.permutation(np.resize(levels, k // 32))).repeat(32)
    a = np.empty((k // 512, 16))
    for p in range(k // 512):
        a[p, :8] = np.random.permutation(np.resize(levels, 8))
        for g in range(8):
            far = levels[np.abs(levels - a[p, g]) >= 10]
            a[p, g + 8] = far[np.random.randint(len(far))]
    return np.exp2(a.ravel()).repeat(32)


BF16 = ml_dtypes.bfloat16


def bf(x):
    return np.asarray(x, np.float32).astype(BF16)


def f64(x):
    return np.asarray(x).astype(np.float64)


B, S, IN_DIM, UNITS = 2, 256, 16384, 512
EPS = 1e-6


def _ternary_kernel():
    limit = np.sqrt(6.0 / (IN_DIM + UNITS))
    w = np.random.uniform(-limit, limit, (IN_DIM, UNITS))
    scale = np.mean(np.abs(w)) + EPS
    return np.clip(np.round(w / scale), -1.0, 1.0)


def setup_inputs():
    s = mx_kscale(IN_DIM)
    return {"x": bf(np.random.standard_normal((B, S, IN_DIM)) * (1.2 / np.sqrt(IN_DIM)) * s),
            "kernel": bf(_ternary_kernel() / s[:, None]),
            "bias": bf(np.random.standard_normal(UNITS) * 0.1)}


def reference(x, kernel, bias):
    return (mxq(f64(x), 2, "e4m3") @ mxq(f64(kernel), 0, "e4m3")) + f64(bias)

@@ -1,0 +1,208 @@
+from contextlib import ExitStack
+
+import concourse.mybir as mybir
+from concourse.masks import make_identity
+
+F32 = mybir.dt.float32
+BF16 = mybir.dt.bfloat16
+U32 = mybir.dt.uint32
+U8 = mybir.dt.uint8
+FP8X4 = mybir.dt.float8_e4m3fn_x4
+
+P = 128
+PACK = 4
+PAIRS = 2
+K_PASS = P * PACK
+ROWS = 512
+K = 16384
+N = 512
+M_TILES = ROWS // P
+PASSES = K // K_PASS
+CHUNK_PASSES = 4
+CHUNK_K = CHUNK_PASSES * K_PASS
+UNITS = M_TILES * (PASSES // CHUNK_PASSES)
+BANK_PASSES = 2
+UNIT_BANKS = CHUNK_PASSES // BANK_PASSES
+
+QUANTISE_AHEAD = M_TILES - 1
+COPY_AHEAD = QUANTISE_AHEAD + 1
+TRANSPOSE_AHEAD = COPY_AHEAD + 1
+X_BUFS = 8
+GROUPS_AHEAD = X_BUFS + TRANSPOSE_AHEAD - QUANTISE_AHEAD
+W_BUFS = GROUPS_AHEAD
+SCALAR_COLS = 192
+
+FLOPS = 2 * ROWS * K * N
+
+
+def tile_bitlinear_k_kernel(tc, x, kernel, bias, out):
+    nc = tc.nc
+    x_rows = x.flatten_outer_dims()
+    out_rows = out.flatten_outer_dims()
+
+    with ExitStack() as ctx:
+        const = ctx.enter_context(tc.tile_pool(name="const", bufs=1))
+        x_loaded = ctx.enter_context(tc.tile_pool(name="x_loaded", bufs=X_BUFS))
+        w_loaded = ctx.enter_context(tc.tile_pool(name="w_loaded", bufs=W_BUFS))
+        grouped = ctx.enter_context(tc.tile_pool(name="grouped", bufs=3))
+        w_quant = ctx.enter_context(tc.tile_pool(name="w_quant", bufs=3))
+        x_quant = ctx.enter_context(tc.tile_pool(name="x_quant", bufs=2 * M_TILES))
+        results = ctx.enter_context(tc.tile_pool(name="results", bufs=M_TILES))
+        psum_t = ctx.enter_context(tc.psum_pool(name="psum_t", bufs=2 * UNIT_BANKS))
+        psum_acc = ctx.enter_context(tc.psum_pool(name="psum_acc", bufs=1))
+        ctx.enter_context(tc.manual_schedule())
+
+        x_raw_of = {}
+        w_raw_of = {}
+        banks_of = {}
+        x_grouped_of = {}
+        w_grouped_of = {}
+        x_codes_of = {}
+        x_scales_of = {}
+        w_codes_of = {}
+        w_scales_of = {}
+
+        def load_x(unit):
+            chunk, m = divmod(unit, M_TILES)
+            x_raw = x_loaded.tile([P, CHUNK_K], BF16)
+            nc.sync.dma_start(
+                out=x_raw[:],
+                in_=x_rows[m * P : (m + 1) * P, chunk * CHUNK_K : (chunk + 1) * CHUNK_K],
+            )
+            x_raw_of[unit] = x_raw
+
+        def load_w(g):
+            w_raw = w_loaded.tile([P, PACK, N], BF16)
+            nc.sync.dma_start(
+                out=w_raw[:],
+                in_=kernel[g * K_PASS : (g + 1) * K_PASS, :].rearrange("(p t) n -> p t n", t=PACK),
+            )
+            w_raw_of[g] = w_raw
+
+        def load_group(g):
+            if 0 <= g + QUANTISE_AHEAD < UNITS:
+                load_x(g + QUANTISE_AHEAD)
+            if 0 <= g < PASSES:
+                load_w(g)
+
+        def transpose_x(unit):
+            words = x_raw_of[unit][:].bitcast(F32)
+            banks = []
+            for b in range(UNIT_BANKS):
+                bank = psum_t.tile([P, BANK_PASSES, PAIRS, P], F32)
+                for a in range(BANK_PASSES):
+                    first = (b * BANK_PASSES + a) * PAIRS * P
+                    for u in range(PAIRS):
+                        nc.tensor.transpose(
+                            bank[:, a, u, :],
+                            words[:, first + u : first + PAIRS * P : PAIRS],
+                            ident[:],
+                        )
+                banks.append(bank)
+            banks_of[unit] = banks
+
+        def copy_x(unit):
+            x_grouped = grouped.tile([P, CHUNK_PASSES, P, PACK], BF16, align_bytes=64)
+            for b in range(UNIT_BANKS):
+                nc.scalar.copy(
+                    out=x_grouped[:, b * BANK_PASSES : (b + 1) * BANK_PASSES].bitcast(F32),
+                    in_=banks_of[unit][b][:].rearrange("p a u r -> p a r u"),
+                )
+            x_grouped_of[unit] = x_grouped
+
+        def quantise_x(unit):
+            x_codes = x_quant.tile([P, CHUNK_PASSES, P], U32, align_bytes=64)
+            x_scales = x_quant.tile([P, CHUNK_PASSES, P], U8, align_bytes=64)
+            nc.vector.quantize_mx(
+                out=x_codes[:].rearrange("p a r -> p (a r)").bitcast(FP8X4),
+                scales=x_scales[:].rearrange("p a r -> p (a r)"),
+                in_=x_grouped_of[unit][:].rearrange("p a r t -> p (a r t)"),
+            )
+            x_codes_of[unit] = x_codes
+            x_scales_of[unit] = x_scales
+
+        def regroup_w(g):
+            w_raw = w_raw_of[g]
+            w_grouped = grouped.tile([P, N, PACK], BF16, align_bytes=64)
+            nc.scalar.copy(
+                out=w_grouped[:, :SCALAR_COLS, :].rearrange("p (c j) t -> p c t j", j=4),
+                in_=w_raw[:, :, :SCALAR_COLS].rearrange("p t (c j) -> p c t j", j=4),
+            )
+            nc.vector.tensor_copy(
+                out=w_grouped[:, SCALAR_COLS:, :].rearrange("p (c j) t -> p c t j", j=4),
+                in_=w_raw[:, :, SCALAR_COLS:].rearrange("p t (c j) -> p c t j", j=4),
+            )
+            w_grouped_of[g] = w_grouped
+
+        def quantise_w(g):
+            w_codes = w_quant.tile([P, N], U32, align_bytes=64)
+            w_scales = w_quant.tile([P, N], U8, align_bytes=64)
+            nc.vector.quantize_mx(
+                out=w_codes[:].bitcast(FP8X4),
+                scales=w_scales[:],
+                in_=w_grouped_of[g][:].rearrange("p n t -> p (n t)"),
+            )
+            w_codes_of[g] = w_codes
+            w_scales_of[g] = w_scales
+
+        def multiply(g):
+            chunk, a = divmod(g, CHUNK_PASSES)
+            for m in range(M_TILES):
+                unit = chunk * M_TILES + m
+                nc.tensor.matmul_mx(
+                    out=acc[m][:],
+                    lhsT=x_codes_of[unit][:, a, :].bitcast(FP8X4),
+                    lhsT_scale=x_scales_of[unit][:, a, :],
+                    rhs=w_codes_of[g][:].bitcast(FP8X4),
+                    rhs_scale=w_scales_of[g][:],
+                    start=(g == 0),
+                    stop=(g == PASSES - 1),
+                )
+
+        def step(n):
+            if n + TRANSPOSE_AHEAD < UNITS:
+                transpose_x(n + TRANSPOSE_AHEAD)
+            if n >= 0:
+                regroup_w(n)
+            if 0 <= n + COPY_AHEAD < UNITS:
+                copy_x(n + COPY_AHEAD)
+            if 0 <= n + QUANTISE_AHEAD < UNITS:
+                quantise_x(n + QUANTISE_AHEAD)
+            if n >= 0:
+                quantise_w(n)
+                multiply(n)
+            load_group(n + GROUPS_AHEAD)
+
+        first_step = -TRANSPOSE_AHEAD
+        for g in range(first_step, first_step + GROUPS_AHEAD):
+            load_group(g)
+
+        ident = const.tile([P, P], F32)
+        make_identity(nc, ident[:])
+        ones = const.tile([P, P], BF16)
+        nc.vector.memset(ones[:], 1.0)
+        bias_row = const.tile([P, N], BF16)
+        nc.vector.memset(bias_row[:], 0.0)
+        nc.scalar.dma_start(out=bias_row[0:1, :], in_=bias.rearrange("(o n) -> o n", o=1))
+
+        acc = []
+        for m in range(M_TILES):
+            acc_m = psum_acc.tile([P, N], F32, name="acc%d" % m)
+            acc.append(acc_m)
+
+        for n in range(first_step, 0):
+            step(n)
+
+        nc.tensor.matmul(out=acc[0][:], lhsT=ones[:], rhs=bias_row[:], start=True, stop=True)
+        bias_all = const.tile([P, N], F32)
+        nc.vector.tensor_copy(out=bias_all[:], in_=acc[0][:])
+
+        for n in range(PASSES):
+            step(n)
+
+        for m in range(M_TILES):
+            result = results.tile([P, N], F32)
+            nc.vector.tensor_tensor(
+                out=result[:], in0=acc[m][:], in1=bias_all[:], op=mybir.AluOpType.add
+            )
+            nc.sync.dma_start(out=out_rows[m * P : (m + 1) * P, :], in_=result[:])

@@ -24,12 +24,14 @@ UNITS = M_TILES * (PASSES // CHUNK_PASSES)
 BANK_PASSES = 2
 UNIT_BANKS = CHUNK_PASSES // BANK_PASSES
 
+RUN = 2
+TRANSPOSE_AHEAD = M_TILES
 QUANTISE_AHEAD = M_TILES - 1
-COPY_AHEAD = QUANTISE_AHEAD + 1
-TRANSPOSE_AHEAD = COPY_AHEAD + 1
-X_BUFS = 8
-GROUPS_AHEAD = X_BUFS + TRANSPOSE_AHEAD - QUANTISE_AHEAD
-W_BUFS = GROUPS_AHEAD
+WEIGHTS_AHEAD = 1
+X_BUFS = 12
+W_BUFS = 12
+X_AHEAD = M_TILES - 1
+GROUPS_AHEAD = W_BUFS + WEIGHTS_AHEAD
 SCALAR_COLS = 192
 
 FLOPS = 2 * ROWS * K * N
@@ -45,8 +47,8 @@ def tile_bitlinear_k_kernel(tc, x, kernel, bias, out):
         x_loaded = ctx.enter_context(tc.tile_pool(name="x_loaded", bufs=X_BUFS))
         w_loaded = ctx.enter_context(tc.tile_pool(name="w_loaded", bufs=W_BUFS))
         grouped = ctx.enter_context(tc.tile_pool(name="grouped", bufs=3))
-        w_quant = ctx.enter_context(tc.tile_pool(name="w_quant", bufs=3))
-        x_quant = ctx.enter_context(tc.tile_pool(name="x_quant", bufs=2 * M_TILES))
+        w_quant = ctx.enter_context(tc.tile_pool(name="w_quant", bufs=4))
+        x_quant = ctx.enter_context(tc.tile_pool(name="x_quant", bufs=2 * M_TILES + RUN))
         results = ctx.enter_context(tc.tile_pool(name="results", bufs=M_TILES))
         psum_t = ctx.enter_context(tc.psum_pool(name="psum_t", bufs=2 * UNIT_BANKS))
         psum_acc = ctx.enter_context(tc.psum_pool(name="psum_acc", bufs=1))
@@ -80,8 +82,8 @@ def tile_bitlinear_k_kernel(tc, x, kernel, bias, out):
             w_raw_of[g] = w_raw
 
         def load_group(g):
-            if 0 <= g + QUANTISE_AHEAD < UNITS:
-                load_x(g + QUANTISE_AHEAD)
+            if 0 <= g + X_AHEAD < UNITS:
+                load_x(g + X_AHEAD)
             if 0 <= g < PASSES:
                 load_w(g)
 
@@ -160,21 +162,27 @@ def tile_bitlinear_k_kernel(tc, x, kernel, bias, out):
                 )
 
         def step(n):
-            if n + TRANSPOSE_AHEAD < UNITS:
-                transpose_x(n + TRANSPOSE_AHEAD)
-            if n >= 0:
-                regroup_w(n)
-            if 0 <= n + COPY_AHEAD < UNITS:
-                copy_x(n + COPY_AHEAD)
-            if 0 <= n + QUANTISE_AHEAD < UNITS:
-                quantise_x(n + QUANTISE_AHEAD)
-            if n >= 0:
-                quantise_w(n)
-                multiply(n)
-            load_group(n + GROUPS_AHEAD)
+            units = range(n + TRANSPOSE_AHEAD, n + TRANSPOSE_AHEAD + RUN)
+            for unit in units:
+                if unit < UNITS:
+                    transpose_x(unit)
+            for i in range(n, n + RUN):
+                if 0 <= i + WEIGHTS_AHEAD < PASSES:
+                    regroup_w(i + WEIGHTS_AHEAD)
+                if i + TRANSPOSE_AHEAD < UNITS:
+                    copy_x(i + TRANSPOSE_AHEAD)
+                if 0 <= i + QUANTISE_AHEAD < UNITS:
+                    quantise_x(i + QUANTISE_AHEAD)
+                if 0 <= i + WEIGHTS_AHEAD < PASSES:
+                    quantise_w(i + WEIGHTS_AHEAD)
+            for g in range(n, n + RUN):
+                if g >= 0:
+                    multiply(g)
+            for g in range(n, n + RUN):
+                load_group(g + GROUPS_AHEAD)
 
         first_step = -TRANSPOSE_AHEAD
-        for g in range(first_step, first_step + GROUPS_AHEAD):
+        for g in range(-X_AHEAD, first_step + GROUPS_AHEAD):
             load_group(g)
 
         ident = const.tile([P, P], F32)
@@ -190,14 +198,14 @@ def tile_bitlinear_k_kernel(tc, x, kernel, bias, out):
             acc_m = psum_acc.tile([P, N], F32, name="acc%d" % m)
             acc.append(acc_m)
 
-        for n in range(first_step, 0):
+        for n in range(first_step, 0, RUN):
             step(n)
 
         nc.tensor.matmul(out=acc[0][:], lhsT=ones[:], rhs=bias_row[:], start=True, stop=True)
         bias_all = const.tile([P, N], F32)
         nc.vector.tensor_copy(out=bias_all[:], in_=acc[0][:])
 
-        for n in range(PASSES):
+        for n in range(0, PASSES, RUN):
             step(n)
 
         for m in range(M_TILES):

@@ -25,13 +25,14 @@ BANK_PASSES = 2
 UNIT_BANKS = CHUNK_PASSES // BANK_PASSES
 
 RUN = 2
-TRANSPOSE_AHEAD = M_TILES
-QUANTISE_AHEAD = M_TILES - 1
-WEIGHTS_AHEAD = 1
-X_BUFS = 12
+TILES_NOW = (0, 1)
+TILES_LATE = (2, 3)
+TRANSPOSE_AHEAD = RUN
+X_BUFS = 11
 W_BUFS = 12
-X_AHEAD = M_TILES - 1
-GROUPS_AHEAD = W_BUFS + WEIGHTS_AHEAD
+X_AHEAD = 1
+GROUPS_AHEAD = W_BUFS
+BIAS_STEP = 4
 SCALAR_COLS = 192
 
 FLOPS = 2 * ROWS * K * N
@@ -46,9 +47,10 @@ def tile_bitlinear_k_kernel(tc, x, kernel, bias, out):
         const = ctx.enter_context(tc.tile_pool(name="const", bufs=1))
         x_loaded = ctx.enter_context(tc.tile_pool(name="x_loaded", bufs=X_BUFS))
         w_loaded = ctx.enter_context(tc.tile_pool(name="w_loaded", bufs=W_BUFS))
-        grouped = ctx.enter_context(tc.tile_pool(name="grouped", bufs=3))
-        w_quant = ctx.enter_context(tc.tile_pool(name="w_quant", bufs=4))
-        x_quant = ctx.enter_context(tc.tile_pool(name="x_quant", bufs=2 * M_TILES + RUN))
+        x_pool = ctx.enter_context(tc.tile_pool(name="x_pool", bufs=2 * RUN + 1))
+        w_pool = ctx.enter_context(tc.tile_pool(name="w_pool", bufs=2 * RUN))
+        w_quant = ctx.enter_context(tc.tile_pool(name="w_quant", bufs=3 * RUN))
+        x_quant = ctx.enter_context(tc.tile_pool(name="x_quant", bufs=2 * M_TILES + 1))
         results = ctx.enter_context(tc.tile_pool(name="results", bufs=M_TILES))
         psum_t = ctx.enter_context(tc.psum_pool(name="psum_t", bufs=2 * UNIT_BANKS))
         psum_acc = ctx.enter_context(tc.psum_pool(name="psum_acc", bufs=1))
@@ -104,7 +106,7 @@ def tile_bitlinear_k_kernel(tc, x, kernel, bias, out):
             banks_of[unit] = banks
 
         def copy_x(unit):
-            x_grouped = grouped.tile([P, CHUNK_PASSES, P, PACK], BF16, align_bytes=64)
+            x_grouped = x_pool.tile([P, CHUNK_PASSES, P, PACK], BF16, align_bytes=64)
             for b in range(UNIT_BANKS):
                 nc.scalar.copy(
                     out=x_grouped[:, b * BANK_PASSES : (b + 1) * BANK_PASSES].bitcast(F32),
@@ -125,7 +127,7 @@ def tile_bitlinear_k_kernel(tc, x, kernel, bias, out):
 
         def regroup_w(g):
             w_raw = w_raw_of[g]
-            w_grouped = grouped.tile([P, N, PACK], BF16, align_bytes=64)
+            w_grouped = w_pool.tile([P, N, PACK], BF16, align_bytes=64)
             nc.scalar.copy(
                 out=w_grouped[:, :SCALAR_COLS, :].rearrange("p (c j) t -> p c t j", j=4),
                 in_=w_raw[:, :, :SCALAR_COLS].rearrange("p t (c j) -> p c t j", j=4),
@@ -147,9 +149,11 @@ def tile_bitlinear_k_kernel(tc, x, kernel, bias, out):
             w_codes_of[g] = w_codes
             w_scales_of[g] = w_scales
 
-        def multiply(g):
+        def multiply(g, tiles):
+            if not 0 <= g < PASSES:
+                return
             chunk, a = divmod(g, CHUNK_PASSES)
-            for m in range(M_TILES):
+            for m in tiles:
                 unit = chunk * M_TILES + m
                 nc.tensor.matmul_mx(
                     out=acc[m][:],
@@ -161,28 +165,34 @@ def tile_bitlinear_k_kernel(tc, x, kernel, bias, out):
                     stop=(g == PASSES - 1),
                 )
 
+        def finish(m):
+            result = results.tile([P, N], F32)
+            nc.vector.tensor_tensor(
+                out=result[:], in0=acc[m][:], in1=bias_all[:], op=mybir.AluOpType.add
+            )
+            nc.sync.dma_start(out=out_rows[m * P : (m + 1) * P, :], in_=result[:])
+
         def step(n):
-            units = range(n + TRANSPOSE_AHEAD, n + TRANSPOSE_AHEAD + RUN)
+            units = [u for u in range(n, n + RUN) if 0 <= u < UNITS]
+            passes = [g for g in range(n, n + RUN) if 0 <= g < PASSES]
+            ahead = [u for u in range(n + RUN, n + 2 * RUN) if u < UNITS]
+            for unit in ahead:
+                transpose_x(unit)
             for unit in units:
-                if unit < UNITS:
-                    transpose_x(unit)
-            for i in range(n, n + RUN):
-                if 0 <= i + WEIGHTS_AHEAD < PASSES:
-                    regroup_w(i + WEIGHTS_AHEAD)
-                if i + TRANSPOSE_AHEAD < UNITS:
-                    copy_x(i + TRANSPOSE_AHEAD)
-                if 0 <= i + QUANTISE_AHEAD < UNITS:
-                    quantise_x(i + QUANTISE_AHEAD)
-                if 0 <= i + WEIGHTS_AHEAD < PASSES:
-                    quantise_w(i + WEIGHTS_AHEAD)
+                quantise_x(unit)
+            for g in passes:
+                regroup_w(g)
+                quantise_w(g)
+            for unit in ahead:
+                copy_x(unit)
+            for g in range(n - RUN, n):
+                multiply(g, TILES_LATE)
             for g in range(n, n + RUN):
-                if g >= 0:
-                    multiply(g)
+                multiply(g, TILES_NOW)
             for g in range(n, n + RUN):
                 load_group(g + GROUPS_AHEAD)
 
-        first_step = -TRANSPOSE_AHEAD
-        for g in range(-X_AHEAD, first_step + GROUPS_AHEAD):
+        for g in range(-X_AHEAD, GROUPS_AHEAD - RUN):
             load_group(g)
 
         ident = const.tile([P, P], F32)
@@ -198,19 +208,19 @@ def tile_bitlinear_k_kernel(tc, x, kernel, bias, out):
             acc_m = psum_acc.tile([P, N], F32, name="acc%d" % m)
             acc.append(acc_m)
 
-        for n in range(first_step, 0, RUN):
-            step(n)
-
-        nc.tensor.matmul(out=acc[0][:], lhsT=ones[:], rhs=bias_row[:], start=True, stop=True)
         bias_all = const.tile([P, N], F32)
-        nc.vector.tensor_copy(out=bias_all[:], in_=acc[0][:])
-
-        for n in range(0, PASSES, RUN):
+        for n in range(-TRANSPOSE_AHEAD, PASSES + RUN, RUN):
+            if n == BIAS_STEP + RUN:
+                nc.vector.tensor_copy(out=bias_all[:], in_=bias_bank)
             step(n)
-
-        for m in range(M_TILES):
-            result = results.tile([P, N], F32)
-            nc.vector.tensor_tensor(
-                out=result[:], in0=acc[m][:], in1=bias_all[:], op=mybir.AluOpType.add
-            )
-            nc.sync.dma_start(out=out_rows[m * P : (m + 1) * P, :], in_=result[:])
+            if n == BIAS_STEP:
+                bank = psum_t.tile([P, BANK_PASSES, PAIRS, P], F32)
+                bias_bank = bank[:].rearrange("p a u r -> p (a u r)")
+                nc.tensor.matmul(
+                    out=bias_bank, lhsT=ones[:], rhs=bias_row[:], start=True, stop=True
+                )
+            if n + RUN == PASSES:
+                for m in TILES_NOW:
+                    finish(m)
+        for m in TILES_LATE:
+            finish(m)

@@ -178,10 +178,13 @@ def tile_bitlinear_k_kernel(tc, x, kernel, bias, out):
             ahead = [u for u in range(n + RUN, n + 2 * RUN) if u < UNITS]
             for unit in ahead:
                 transpose_x(unit)
+            for g in passes[:1]:
+                regroup_w(g)
             for unit in units:
                 quantise_x(unit)
-            for g in passes:
+            for g in passes[1:]:
                 regroup_w(g)
+            for g in passes:
                 quantise_w(g)
             for unit in ahead:
                 copy_x(unit)

@@ -195,16 +195,18 @@ def tile_bitlinear_k_kernel(tc, x, kernel, bias, out):
             for g in range(n, n + RUN):
                 load_group(g + GROUPS_AHEAD)
 
-        for g in range(-X_AHEAD, GROUPS_AHEAD - RUN):
-            load_group(g)
-
         ident = const.tile([P, P], F32)
         make_identity(nc, ident[:])
         ones = const.tile([P, P], BF16)
         nc.vector.memset(ones[:], 1.0)
         bias_row = const.tile([P, N], BF16)
         nc.vector.memset(bias_row[:], 0.0)
-        nc.scalar.dma_start(out=bias_row[0:1, :], in_=bias.rearrange("(o n) -> o n", o=1))
+
+        for g in range(-X_AHEAD, RUN):
+            load_group(g)
+        nc.sync.dma_start(out=bias_row[0:1, :], in_=bias.rearrange("(o n) -> o n", o=1))
+        for g in range(RUN, GROUPS_AHEAD - RUN):
+            load_group(g)
 
         acc = []
         for m in range(M_TILES):
@@ -213,9 +215,9 @@ def tile_bitlinear_k_kernel(tc, x, kernel, bias, out):
 
         bias_all = const.tile([P, N], F32)
         for n in range(-TRANSPOSE_AHEAD, PASSES + RUN, RUN):
-            if n == BIAS_STEP + RUN:
-                nc.vector.tensor_copy(out=bias_all[:], in_=bias_bank)
             step(n)
+            if n == BIAS_STEP + RUN:
+                nc.scalar.copy(out=bias_all[:], in_=bias_bank)
             if n == BIAS_STEP:
                 bank = psum_t.tile([P, BANK_PASSES, PAIRS, P], F32)
                 bias_bank = bank[:].rearrange("p a u r -> p (a u r)")

from contextlib import ExitStack

import concourse.mybir as mybir
from concourse.masks import make_identity

F32 = mybir.dt.float32
BF16 = mybir.dt.bfloat16
U32 = mybir.dt.uint32
U8 = mybir.dt.uint8
FP8X4 = mybir.dt.float8_e4m3fn_x4

P = 128
PACK = 4
PAIRS = 2
K_PASS = P * PACK
ROWS = 512
K = 16384
N = 512
M_TILES = ROWS // P
PASSES = K // K_PASS
CHUNK_PASSES = 4
CHUNK_K = CHUNK_PASSES * K_PASS
UNITS = M_TILES * (PASSES // CHUNK_PASSES)
BANK_PASSES = 2
UNIT_BANKS = CHUNK_PASSES // BANK_PASSES

RUN = 2
TILES_NOW = (0, 1)
TILES_LATE = (2, 3)
TRANSPOSE_AHEAD = RUN
X_BUFS = 11
W_BUFS = 12
X_AHEAD = 1
GROUPS_AHEAD = W_BUFS
BIAS_STEP = 4
SCALAR_COLS = 192

FLOPS = 2 * ROWS * K * N


def tile_bitlinear_k_kernel(tc, x, kernel, bias, out):
    nc = tc.nc
    x_rows = x.flatten_outer_dims()
    out_rows = out.flatten_outer_dims()

    with ExitStack() as ctx:
        const = ctx.enter_context(tc.tile_pool(name="const", bufs=1))
        x_loaded = ctx.enter_context(tc.tile_pool(name="x_loaded", bufs=X_BUFS))
        w_loaded = ctx.enter_context(tc.tile_pool(name="w_loaded", bufs=W_BUFS))
        x_pool = ctx.enter_context(tc.tile_pool(name="x_pool", bufs=2 * RUN + 1))
        w_pool = ctx.enter_context(tc.tile_pool(name="w_pool", bufs=2 * RUN))
        w_quant = ctx.enter_context(tc.tile_pool(name="w_quant", bufs=3 * RUN))
        x_quant = ctx.enter_context(tc.tile_pool(name="x_quant", bufs=2 * M_TILES + 1))
        results = ctx.enter_context(tc.tile_pool(name="results", bufs=M_TILES))
        psum_t = ctx.enter_context(tc.psum_pool(name="psum_t", bufs=2 * UNIT_BANKS))
        psum_acc = ctx.enter_context(tc.psum_pool(name="psum_acc", bufs=1))
        ctx.enter_context(tc.manual_schedule())

        x_raw_of = {}
        w_raw_of = {}
        banks_of = {}
        x_grouped_of = {}
        w_grouped_of = {}
        x_codes_of = {}
        x_scales_of = {}
        w_codes_of = {}
        w_scales_of = {}

        def load_x(unit):
            chunk, m = divmod(unit, M_TILES)
            x_raw = x_loaded.tile([P, CHUNK_K], BF16)
            nc.sync.dma_start(
                out=x_raw[:],
                in_=x_rows[m * P : (m + 1) * P, chunk * CHUNK_K : (chunk + 1) * CHUNK_K],
            )
            x_raw_of[unit] = x_raw

        def load_w(g):
            w_raw = w_loaded.tile([P, PACK, N], BF16)
            nc.sync.dma_start(
                out=w_raw[:],
                in_=kernel[g * K_PASS : (g + 1) * K_PASS, :].rearrange("(p t) n -> p t n", t=PACK),
            )
            w_raw_of[g] = w_raw

        def load_group(g):
            if 0 <= g + X_AHEAD < UNITS:
                load_x(g + X_AHEAD)
            if 0 <= g < PASSES:
                load_w(g)

        def transpose_x(unit):
            words = x_raw_of[unit][:].bitcast(F32)
            banks = []
            for b in range(UNIT_BANKS):
                bank = psum_t.tile([P, BANK_PASSES, PAIRS, P], F32)
                for a in range(BANK_PASSES):
                    first = (b * BANK_PASSES + a) * PAIRS * P
                    for u in range(PAIRS):
                        nc.tensor.transpose(
                            bank[:, a, u, :],
                            words[:, first + u : first + PAIRS * P : PAIRS],
                            ident[:],
                        )
                banks.append(bank)
            banks_of[unit] = banks

        def copy_x(unit):
            x_grouped = x_pool.tile([P, CHUNK_PASSES, P, PACK], BF16, align_bytes=64)
            for b in range(UNIT_BANKS):
                nc.scalar.copy(
                    out=x_grouped[:, b * BANK_PASSES : (b + 1) * BANK_PASSES].bitcast(F32),
                    in_=banks_of[unit][b][:].rearrange("p a u r -> p a r u"),
                )
            x_grouped_of[unit] = x_grouped

        def quantise_x(unit):
            x_codes = x_quant.tile([P, CHUNK_PASSES, P], U32, align_bytes=64)
            x_scales = x_quant.tile([P, CHUNK_PASSES, P], U8, align_bytes=64)
            nc.vector.quantize_mx(
                out=x_codes[:].rearrange("p a r -> p (a r)").bitcast(FP8X4),
                scales=x_scales[:].rearrange("p a r -> p (a r)"),
                in_=x_grouped_of[unit][:].rearrange("p a r t -> p (a r t)"),
            )
            x_codes_of[unit] = x_codes
            x_scales_of[unit] = x_scales

        def regroup_w(g):
            w_raw = w_raw_of[g]
            w_grouped = w_pool.tile([P, N, PACK], BF16, align_bytes=64)
            nc.scalar.copy(
                out=w_grouped[:, :SCALAR_COLS, :].rearrange("p (c j) t -> p c t j", j=4),
                in_=w_raw[:, :, :SCALAR_COLS].rearrange("p t (c j) -> p c t j", j=4),
            )
            nc.vector.tensor_copy(
                out=w_grouped[:, SCALAR_COLS:, :].rearrange("p (c j) t -> p c t j", j=4),
                in_=w_raw[:, :, SCALAR_COLS:].rearrange("p t (c j) -> p c t j", j=4),
            )
            w_grouped_of[g] = w_grouped

        def quantise_w(g):
            w_codes = w_quant.tile([P, N], U32, align_bytes=64)
            w_scales = w_quant.tile([P, N], U8, align_bytes=64)
            nc.vector.quantize_mx(
                out=w_codes[:].bitcast(FP8X4),
                scales=w_scales[:],
                in_=w_grouped_of[g][:].rearrange("p n t -> p (n t)"),
            )
            w_codes_of[g] = w_codes
            w_scales_of[g] = w_scales

        def multiply(g, tiles):
            if not 0 <= g < PASSES:
                return
            chunk, a = divmod(g, CHUNK_PASSES)
            for m in tiles:
                unit = chunk * M_TILES + m
                nc.tensor.matmul_mx(
                    out=acc[m][:],
                    lhsT=x_codes_of[unit][:, a, :].bitcast(FP8X4),
                    lhsT_scale=x_scales_of[unit][:, a, :],
                    rhs=w_codes_of[g][:].bitcast(FP8X4),
                    rhs_scale=w_scales_of[g][:],
                    start=(g == 0),
                    stop=(g == PASSES - 1),
                )

        def finish(m):
            result = results.tile([P, N], F32)
            nc.vector.tensor_tensor(
                out=result[:], in0=acc[m][:], in1=bias_all[:], op=mybir.AluOpType.add
            )
            nc.sync.dma_start(out=out_rows[m * P : (m + 1) * P, :], in_=result[:])

        def step(n):
            units = [u for u in range(n, n + RUN) if 0 <= u < UNITS]
            passes = [g for g in range(n, n + RUN) if 0 <= g < PASSES]
            ahead = [u for u in range(n + RUN, n + 2 * RUN) if u < UNITS]
            for unit in ahead:
                transpose_x(unit)
            for g in passes[:1]:
                regroup_w(g)
            for unit in units:
                quantise_x(unit)
            for g in passes[1:]:
                regroup_w(g)
            for g in passes:
                quantise_w(g)
            for unit in ahead:
                copy_x(unit)
            for g in range(n - RUN, n):
                multiply(g, TILES_LATE)
            for g in range(n, n + RUN):
                multiply(g, TILES_NOW)
            for g in range(n, n + RUN):
                load_group(g + GROUPS_AHEAD)

        ident = const.tile([P, P], F32)
        make_identity(nc, ident[:])
        ones = const.tile([P, P], BF16)
        nc.vector.memset(ones[:], 1.0)
        bias_row = const.tile([P, N], BF16)
        nc.vector.memset(bias_row[:], 0.0)

        for g in range(-X_AHEAD, RUN):
            load_group(g)
        nc.sync.dma_start(out=bias_row[0:1, :], in_=bias.rearrange("(o n) -> o n", o=1))
        for g in range(RUN, GROUPS_AHEAD - RUN):
            load_group(g)

        acc = []
        for m in range(M_TILES):
            acc_m = psum_acc.tile([P, N], F32, name="acc%d" % m)
            acc.append(acc_m)

        bias_all = const.tile([P, N], F32)
        for n in range(-TRANSPOSE_AHEAD, PASSES + RUN, RUN):
            step(n)
            if n == BIAS_STEP + RUN:
                nc.scalar.copy(out=bias_all[:], in_=bias_bank)
            if n == BIAS_STEP:
                bank = psum_t.tile([P, BANK_PASSES, PAIRS, P], F32)
                bias_bank = bank[:].rearrange("p a u r -> p (a u r)")
                nc.tensor.matmul(
                    out=bias_bank, lhsT=ones[:], rhs=bias_row[:], start=True, stop=True
                )
            if n + RUN == PASSES:
                for m in TILES_NOW:
                    finish(m)
        for m in TILES_LATE:
            finish(m)
